import numpy as np
import ml_dtypes

BF16 = ml_dtypes.bfloat16


def bf(x):
    return np.asarray(x, np.float32).astype(BF16)


def f32(x):
    return np.asarray(x, np.float32)


def f64(x):
    return np.asarray(x).astype(np.float64)


def striped(idx):
    return np.tile(idx.reshape(-1, 16).T, (8, 1))


X, H, H3, S, N = 256, 256, 768, 512, 256


def sigmoid(v):
    return 1.0 / (1.0 + np.exp(-v))


def setup_inputs():
    return {"base": f32(0.3 * np.random.standard_normal((H, S))), "x": bf(np.random.standard_normal((X, N))), "w_iou": bf(np.random.standard_normal((X, H3)) / np.sqrt(X)), "b_iou": f32(0.1 * np.random.standard_normal((H3, 1))), "offs": striped(np.random.permutation(S)[:N])}


def reference(base, x, w_iou, b_iou, offs):
    idx = offs[:16].T.reshape(-1)
    iou = f64(w_iou).T @ f64(x) + f64(b_iou)
    p_i, p_o, p_u = iou[:H], iou[H:H + H], iou[H + H:]
    cell = sigmoid(p_i) * np.tanh(p_u)
    out = f64(base).copy()
    out[:, idx] = sigmoid(p_o) * np.tanh(cell)
    return out

@@ -1,0 +1,68 @@
+import concourse.mybir as mybir
+
+BF16, F32, U16 = mybir.dt.bfloat16, mybir.dt.float32, mybir.dt.uint16
+SIGMOID = mybir.ActivationFunctionType.Sigmoid
+TANH = mybir.ActivationFunctionType.Tanh
+MULT = mybir.AluOpType.mult
+
+P = 128
+X = 256
+H = 256
+S = 512
+N = 256
+K_BLOCKS = X // P
+C_BLOCKS = H // P
+GATE_I, GATE_O, GATE_U = 0, 1, 2
+
+FLOPS = 2 * X * 3 * H * N
+
+
+def tile_treemodel_s_kernel(tc, base, x, w_iou, b_iou, offs, out):
+    nc = tc.nc
+    with (
+        tc.tile_pool(name="held", bufs=1) as held,
+        tc.tile_pool(name="work", bufs=2) as work,
+        tc.psum_pool(name="psum", bufs=2) as psum,
+    ):
+        offsets = held.tile([P, N // 16], U16, name="offsets")
+        bias = held.tile([P, 3 * C_BLOCKS], F32, name="bias")
+        x_sb = [held.tile([P, N], BF16, name=f"x_sb{k}") for k in range(K_BLOCKS)]
+        w_sb = [held.tile([P, 3 * H], BF16, name=f"w_sb{k}") for k in range(K_BLOCKS)]
+        window = [held.tile([P, S], F32, name=f"window{c}") for c in range(C_BLOCKS)]
+
+        with nc.allow_non_contiguous_dma(reason="768 biases, one to a partition and column"):
+            nc.scalar.dma_start(bias[:], b_iou.rearrange("(g p) o -> p (g o)", p=P))
+        queues = (nc.sync, nc.scalar)
+        for k in range(K_BLOCKS):
+            queues[k].dma_start(x_sb[k][:], x[k * P : (k + 1) * P, :])
+            queues[k].dma_start(w_sb[k][:], w_iou[k * P : (k + 1) * P, :])
+        nc.sync.dma_start(offsets[:], offs)
+        for c in range(C_BLOCKS):
+            queues[c].dma_start(window[c][:], base[c * P : (c + 1) * P, :])
+
+        for c in range(C_BLOCKS):
+
+            def gate(g, func, name):
+                pre = psum.tile([P, N], F32, name="pre_" + name)
+                first = g * H + c * P
+                for k in range(K_BLOCKS):
+                    nc.tensor.matmul(
+                        pre[:], w_sb[k][:, first : first + P], x_sb[k][:],
+                        start=(k == 0), stop=(k == K_BLOCKS - 1),
+                    )
+                act = work.tile([P, N], F32, name=name)
+                column = g * C_BLOCKS + c
+                nc.scalar.activation(act[:], pre[:], func, bias=bias[:, column : column + 1])
+                return act
+
+            sig_i = gate(GATE_I, SIGMOID, "sig_i")
+            tanh_u = gate(GATE_U, TANH, "tanh_u")
+            sig_o = gate(GATE_O, SIGMOID, "sig_o")
+
+            cell = work.tile([P, N], F32, name="cell")
+            nc.vector.tensor_tensor(cell[:], sig_i[:], tanh_u[:], MULT)
+            tanh_cell = work.tile([P, N], F32, name="tanh_cell")
+            nc.scalar.activation(tanh_cell[:], cell[:], TANH)
+
+            nc.vector.tensor_tensor(window[c][:].indirect(offsets[:]), sig_o[:], tanh_cell[:], MULT)
+            nc.sync.dma_start(out[c * P : (c + 1) * P, :], window[c][:])

@@ -26,28 +26,32 @@ def tile_treemodel_s_kernel(tc, base, x, w_iou, b_iou, offs, out):
     ):
         offsets = held.tile([P, N // 16], U16, name="offsets")
         bias = held.tile([P, 3 * C_BLOCKS], F32, name="bias")
-        x_sb = [held.tile([P, N], BF16, name=f"x_sb{k}") for k in range(K_BLOCKS)]
-        w_sb = [held.tile([P, 3 * H], BF16, name=f"w_sb{k}") for k in range(K_BLOCKS)]
+        x_sb = held.tile([P, K_BLOCKS, N], BF16, name="x_sb")
+        w_sb = [held.tile([P, K_BLOCKS, H], BF16, name=f"w_sb{g}") for g in range(3)]
         window = [held.tile([P, S], F32, name=f"window{c}") for c in range(C_BLOCKS)]
 
         with nc.allow_non_contiguous_dma(reason="768 biases, one to a partition and column"):
             nc.scalar.dma_start(bias[:], b_iou.rearrange("(g p) o -> p (g o)", p=P))
-        queues = (nc.sync, nc.scalar)
-        for k in range(K_BLOCKS):
-            queues[k].dma_start(x_sb[k][:], x[k * P : (k + 1) * P, :])
-            queues[k].dma_start(w_sb[k][:], w_iou[k * P : (k + 1) * P, :])
+
+        warm = held.tile([P, 1], F32, name="warm")
+        nc.vector.memset(warm[:], 0.0)
+        nc.scalar.activation(warm[:], warm[:], SIGMOID)
+
+        w_blocks = w_iou.rearrange("(k p) c -> p k c", p=P)
+        nc.sync.dma_start(x_sb[:], x.rearrange("(k p) j -> p k j", p=P))
+        for g in (GATE_I, GATE_U, GATE_O):
+            nc.sync.dma_start(w_sb[g][:], w_blocks[:, :, g * H : (g + 1) * H])
         nc.sync.dma_start(offsets[:], offs)
         for c in range(C_BLOCKS):
-            queues[c].dma_start(window[c][:], base[c * P : (c + 1) * P, :])
+            nc.sync.dma_start(window[c][:], base[c * P : (c + 1) * P, :])
 
         for c in range(C_BLOCKS):
 
             def gate(g, func, name):
                 pre = psum.tile([P, N], F32, name="pre_" + name)
-                first = g * H + c * P
                 for k in range(K_BLOCKS):
                     nc.tensor.matmul(
-                        pre[:], w_sb[k][:, first : first + P], x_sb[k][:],
+                        pre[:], w_sb[g][:, k, c * P : (c + 1) * P], x_sb[:, k, :],
                         start=(k == 0), stop=(k == K_BLOCKS - 1),
                     )
                 act = work.tile([P, N], F32, name=name)

@@ -15,13 +15,16 @@ C_BLOCKS = H // P
 GATE_I, GATE_O, GATE_U = 0, 1, 2
 
 FLOPS = 2 * X * 3 * H * N
+HALVES = 2
+M = N // HALVES
 
 
 def tile_treemodel_s_kernel(tc, base, x, w_iou, b_iou, offs, out):
     nc = tc.nc
+    pieces = [(c, h) for c in range(C_BLOCKS) for h in range(HALVES)]
     with (
         tc.tile_pool(name="held", bufs=1) as held,
-        tc.tile_pool(name="work", bufs=2) as work,
+        tc.tile_pool(name="work", bufs=len(pieces)) as work,
         tc.psum_pool(name="psum", bufs=2) as psum,
     ):
         offsets = held.tile([P, N // 16], U16, name="offsets")
@@ -45,28 +48,37 @@ def tile_treemodel_s_kernel(tc, base, x, w_iou, b_iou, offs, out):
         for c in range(C_BLOCKS):
             nc.sync.dma_start(window[c][:], base[c * P : (c + 1) * P, :])
 
-        for c in range(C_BLOCKS):
+        def gate(c, h, g, func, name):
+            pre = psum.tile([P, M], F32, name="pre_" + name)
+            for k in range(K_BLOCKS):
+                nc.tensor.matmul(
+                    pre[:], w_sb[g][:, k, c * P : (c + 1) * P], x_sb[:, k, h * M : (h + 1) * M],
+                    start=(k == 0), stop=(k == K_BLOCKS - 1),
+                )
+            act = work.tile([P, M], F32, name=name)
+            column = g * C_BLOCKS + c
+            nc.scalar.activation(act[:], pre[:], func, bias=bias[:, column : column + 1])
+            return act
 
-            def gate(g, func, name):
-                pre = psum.tile([P, N], F32, name="pre_" + name)
-                for k in range(K_BLOCKS):
-                    nc.tensor.matmul(
-                        pre[:], w_sb[g][:, k, c * P : (c + 1) * P], x_sb[:, k, :],
-                        start=(k == 0), stop=(k == K_BLOCKS - 1),
-                    )
-                act = work.tile([P, N], F32, name=name)
-                column = g * C_BLOCKS + c
-                nc.scalar.activation(act[:], pre[:], func, bias=bias[:, column : column + 1])
-                return act
-
-            sig_i = gate(GATE_I, SIGMOID, "sig_i")
-            tanh_u = gate(GATE_U, TANH, "tanh_u")
-            sig_o = gate(GATE_O, SIGMOID, "sig_o")
-
-            cell = work.tile([P, N], F32, name="cell")
+        def gates_and_cell(c, h):
+            sig_i = gate(c, h, GATE_I, SIGMOID, "sig_i")
+            tanh_u = gate(c, h, GATE_U, TANH, "tanh_u")
+            cell = work.tile([P, M], F32, name="cell")
             nc.vector.tensor_tensor(cell[:], sig_i[:], tanh_u[:], MULT)
-            tanh_cell = work.tile([P, N], F32, name="tanh_cell")
-            nc.scalar.activation(tanh_cell[:], cell[:], TANH)
+            sig_o = gate(c, h, GATE_O, SIGMOID, "sig_o")
+            return sig_o, cell
 
-            nc.vector.tensor_tensor(window[c][:].indirect(offsets[:]), sig_o[:], tanh_cell[:], MULT)
-            nc.sync.dma_start(out[c * P : (c + 1) * P, :], window[c][:])
+        def place(c, h, sig_o, cell):
+            tanh_cell = work.tile([P, M], F32, name="tanh_cell")
+            nc.scalar.activation(tanh_cell[:], cell[:], TANH)
+            piece_offsets = offsets[:, h * (M // 16) : (h + 1) * (M // 16)]
+            nc.vector.tensor_tensor(window[c][:].indirect(piece_offsets), sig_o[:], tanh_cell[:], MULT)
+            if h == HALVES - 1:
+                nc.sync.dma_start(out[c * P : (c + 1) * P, :], window[c][:])
+
+        ahead = gates_and_cell(*pieces[0])
+        for i, piece in enumerate(pieces):
+            current = ahead
+            if i + 1 < len(pieces):
+                ahead = gates_and_cell(*pieces[i + 1])
+            place(*piece, *current)

@@ -1,4 +1,5 @@
 import concourse.mybir as mybir
+from concourse.masks import make_identity
 
 BF16, F32, U16 = mybir.dt.bfloat16, mybir.dt.float32, mybir.dt.uint16
 SIGMOID = mybir.ActivationFunctionType.Sigmoid
@@ -13,6 +14,7 @@ N = 256
 K_BLOCKS = X // P
 C_BLOCKS = H // P
 GATE_I, GATE_O, GATE_U = 0, 1, 2
+B_ROWS = 3 * C_BLOCKS
 
 FLOPS = 2 * X * 3 * H * N
 HALVES = 2
@@ -26,19 +28,26 @@ def tile_treemodel_s_kernel(tc, base, x, w_iou, b_iou, offs, out):
         tc.tile_pool(name="held", bufs=1) as held,
         tc.tile_pool(name="work", bufs=len(pieces)) as work,
         tc.psum_pool(name="psum", bufs=2) as psum,
+        tc.psum_pool(name="psum_bias", bufs=1) as psum_bias,
     ):
         offsets = held.tile([P, N // 16], U16, name="offsets")
-        bias = held.tile([P, 3 * C_BLOCKS], F32, name="bias")
         x_sb = held.tile([P, K_BLOCKS, N], BF16, name="x_sb")
         w_sb = [held.tile([P, K_BLOCKS, H], BF16, name=f"w_sb{g}") for g in range(3)]
         window = [held.tile([P, S], F32, name=f"window{c}") for c in range(C_BLOCKS)]
 
-        with nc.allow_non_contiguous_dma(reason="768 biases, one to a partition and column"):
-            nc.scalar.dma_start(bias[:], b_iou.rearrange("(g p) o -> p (g o)", p=P))
+        b_rows = held.tile([B_ROWS, P], F32, name="b_rows")
+        nc.scalar.dma_start(b_rows[:], b_iou.rearrange("(r p) o -> r (p o)", p=P))
 
         warm = held.tile([P, 1], F32, name="warm")
         nc.vector.memset(warm[:], 0.0)
         nc.scalar.activation(warm[:], warm[:], SIGMOID)
+
+        identity = held.tile([B_ROWS, B_ROWS], F32, name="identity")
+        make_identity(nc, identity[:])
+        bias_ps = psum_bias.tile([P, B_ROWS], F32, name="bias_ps")
+        nc.tensor.matmul(bias_ps[:], b_rows[:], identity[:], start=True, stop=True)
+        bias = held.tile([P, B_ROWS], F32, name="bias")
+        nc.vector.tensor_copy(bias[:], bias_ps[:])
 
         w_blocks = w_iou.rearrange("(k p) c -> p k c", p=P)
         nc.sync.dma_start(x_sb[:], x.rearrange("(k p) j -> p k j", p=P))

@@ -1,5 +1,4 @@
 import concourse.mybir as mybir
-from concourse.masks import make_identity
 
 BF16, F32, U16 = mybir.dt.bfloat16, mybir.dt.float32, mybir.dt.uint16
 SIGMOID = mybir.ActivationFunctionType.Sigmoid
@@ -14,10 +13,10 @@ N = 256
 K_BLOCKS = X // P
 C_BLOCKS = H // P
 GATE_I, GATE_O, GATE_U = 0, 1, 2
-B_ROWS = 3 * C_BLOCKS
 
 FLOPS = 2 * X * 3 * H * N
 HALVES = 2
+WARM_MATMULS = 16
 M = N // HALVES
 
 
@@ -28,26 +27,26 @@ def tile_treemodel_s_kernel(tc, base, x, w_iou, b_iou, offs, out):
         tc.tile_pool(name="held", bufs=1) as held,
         tc.tile_pool(name="work", bufs=len(pieces)) as work,
         tc.psum_pool(name="psum", bufs=2) as psum,
-        tc.psum_pool(name="psum_bias", bufs=1) as psum_bias,
+        tc.psum_pool(name="psum_idle", bufs=1) as psum_idle,
     ):
         offsets = held.tile([P, N // 16], U16, name="offsets")
+        bias = held.tile([P, 3 * C_BLOCKS], F32, name="bias")
         x_sb = held.tile([P, K_BLOCKS, N], BF16, name="x_sb")
         w_sb = [held.tile([P, K_BLOCKS, H], BF16, name=f"w_sb{g}") for g in range(3)]
         window = [held.tile([P, S], F32, name=f"window{c}") for c in range(C_BLOCKS)]
 
-        b_rows = held.tile([B_ROWS, P], F32, name="b_rows")
-        nc.scalar.dma_start(b_rows[:], b_iou.rearrange("(r p) o -> r (p o)", p=P))
+        with nc.allow_non_contiguous_dma(reason="768 biases, one to a partition and column"):
+            nc.scalar.dma_start(bias[:], b_iou.rearrange("(g p) o -> p (g o)", p=P))
 
         warm = held.tile([P, 1], F32, name="warm")
-        nc.vector.memset(warm[:], 0.0)
+        nc.gpsimd.memset(warm[:], 0.0)
         nc.scalar.activation(warm[:], warm[:], SIGMOID)
 
-        identity = held.tile([B_ROWS, B_ROWS], F32, name="identity")
-        make_identity(nc, identity[:])
-        bias_ps = psum_bias.tile([P, B_ROWS], F32, name="bias_ps")
-        nc.tensor.matmul(bias_ps[:], b_rows[:], identity[:], start=True, stop=True)
-        bias = held.tile([P, B_ROWS], F32, name="bias")
-        nc.vector.tensor_copy(bias[:], bias_ps[:])
+        zeros = held.tile([P, P], BF16, name="zeros")
+        nc.vector.memset(zeros[:], 0.0)
+        idle = psum_idle.tile([P, P], F32, name="idle")
+        for repeat in range(WARM_MATMULS):
+            nc.tensor.matmul(idle[:], zeros[:], zeros[:], start=True, stop=True)
 
         w_blocks = w_iou.rearrange("(k p) c -> p k c", p=P)
         nc.sync.dma_start(x_sb[:], x.rearrange("(k p) j -> p k j", p=P))
@@ -69,15 +68,15 @@ def tile_treemodel_s_kernel(tc, base, x, w_iou, b_iou, offs, out):
             nc.scalar.activation(act[:], pre[:], func, bias=bias[:, column : column + 1])
             return act
 
-        def gates_and_cell(c, h):
+        def make_cell(c, h):
             sig_i = gate(c, h, GATE_I, SIGMOID, "sig_i")
             tanh_u = gate(c, h, GATE_U, TANH, "tanh_u")
             cell = work.tile([P, M], F32, name="cell")
             nc.vector.tensor_tensor(cell[:], sig_i[:], tanh_u[:], MULT)
-            sig_o = gate(c, h, GATE_O, SIGMOID, "sig_o")
-            return sig_o, cell
+            return cell
 
-        def place(c, h, sig_o, cell):
+        def place(c, h, cell):
+            sig_o = gate(c, h, GATE_O, SIGMOID, "sig_o")
             tanh_cell = work.tile([P, M], F32, name="tanh_cell")
             nc.scalar.activation(tanh_cell[:], cell[:], TANH)
             piece_offsets = offsets[:, h * (M // 16) : (h + 1) * (M // 16)]
@@ -85,9 +84,9 @@ def tile_treemodel_s_kernel(tc, base, x, w_iou, b_iou, offs, out):
             if h == HALVES - 1:
                 nc.sync.dma_start(out[c * P : (c + 1) * P, :], window[c][:])
 
-        ahead = gates_and_cell(*pieces[0])
+        ahead = make_cell(*pieces[0])
         for i, piece in enumerate(pieces):
             current = ahead
             if i + 1 < len(pieces):
-                ahead = gates_and_cell(*pieces[i + 1])
-            place(*piece, *current)
+                ahead = make_cell(*pieces[i + 1])
+            place(*piece, current)

@@ -15,7 +15,7 @@ C_BLOCKS = H // P
 GATE_I, GATE_O, GATE_U = 0, 1, 2
 
 FLOPS = 2 * X * 3 * H * N
-HALVES = 2
+HALVES = 1
 WARM_MATMULS = 16
 M = N // HALVES
 

@@ -15,18 +15,16 @@ C_BLOCKS = H // P
 GATE_I, GATE_O, GATE_U = 0, 1, 2
 
 FLOPS = 2 * X * 3 * H * N
-HALVES = 1
+
 WARM_MATMULS = 16
-M = N // HALVES
 
 
 def tile_treemodel_s_kernel(tc, base, x, w_iou, b_iou, offs, out):
     nc = tc.nc
-    pieces = [(c, h) for c in range(C_BLOCKS) for h in range(HALVES)]
     with (
         tc.tile_pool(name="held", bufs=1) as held,
-        tc.tile_pool(name="work", bufs=len(pieces)) as work,
-        tc.psum_pool(name="psum", bufs=2) as psum,
+        tc.tile_pool(name="work", bufs=C_BLOCKS) as work,
+        tc.psum_pool(name="psum", bufs=C_BLOCKS) as psum,
         tc.psum_pool(name="psum_idle", bufs=1) as psum_idle,
     ):
         offsets = held.tile([P, N // 16], U16, name="offsets")
@@ -36,7 +34,7 @@ def tile_treemodel_s_kernel(tc, base, x, w_iou, b_iou, offs, out):
         window = [held.tile([P, S], F32, name=f"window{c}") for c in range(C_BLOCKS)]
 
         with nc.allow_non_contiguous_dma(reason="768 biases, one to a partition and column"):
-            nc.scalar.dma_start(bias[:], b_iou.rearrange("(g p) o -> p (g o)", p=P))
+            nc.scalar.dma_start(bias[:], b_iou.rearrange("(r p) o -> p (r o)", p=P))
 
         warm = held.tile([P, 1], F32, name="warm")
         nc.gpsimd.memset(warm[:], 0.0)
@@ -53,40 +51,36 @@ def tile_treemodel_s_kernel(tc, base, x, w_iou, b_iou, offs, out):
         for g in (GATE_I, GATE_U, GATE_O):
             nc.sync.dma_start(w_sb[g][:], w_blocks[:, :, g * H : (g + 1) * H])
         nc.sync.dma_start(offsets[:], offs)
-        for c in range(C_BLOCKS):
-            nc.sync.dma_start(window[c][:], base[c * P : (c + 1) * P, :])
 
-        def gate(c, h, g, func, name):
-            pre = psum.tile([P, M], F32, name="pre_" + name)
+        for c in range(C_BLOCKS):
+            nc.gpsimd.dma_start(window[c][:], base[c * P : (c + 1) * P, :])
+
+        def gate(c, g, func, name):
+            pre = psum.tile([P, N], F32, name="pre_" + name)
             for k in range(K_BLOCKS):
                 nc.tensor.matmul(
-                    pre[:], w_sb[g][:, k, c * P : (c + 1) * P], x_sb[:, k, h * M : (h + 1) * M],
+                    pre[:], w_sb[g][:, k, c * P : (c + 1) * P], x_sb[:, k, :],
                     start=(k == 0), stop=(k == K_BLOCKS - 1),
                 )
-            act = work.tile([P, M], F32, name=name)
+            act = work.tile([P, N], F32, name=name)
             column = g * C_BLOCKS + c
             nc.scalar.activation(act[:], pre[:], func, bias=bias[:, column : column + 1])
             return act
 
-        def make_cell(c, h):
-            sig_i = gate(c, h, GATE_I, SIGMOID, "sig_i")
-            tanh_u = gate(c, h, GATE_U, TANH, "tanh_u")
-            cell = work.tile([P, M], F32, name="cell")
+        def make_cell(c):
+            sig_i = gate(c, GATE_I, SIGMOID, "sig_i")
+            tanh_u = gate(c, GATE_U, TANH, "tanh_u")
+            cell = work.tile([P, N], F32, name="cell")
             nc.vector.tensor_tensor(cell[:], sig_i[:], tanh_u[:], MULT)
             return cell
 
-        def place(c, h, cell):
-            sig_o = gate(c, h, GATE_O, SIGMOID, "sig_o")
-            tanh_cell = work.tile([P, M], F32, name="tanh_cell")
+        def place(c, cell):
+            sig_o = gate(c, GATE_O, SIGMOID, "sig_o")
+            tanh_cell = work.tile([P, N], F32, name="tanh_cell")
             nc.scalar.activation(tanh_cell[:], cell[:], TANH)
-            piece_offsets = offsets[:, h * (M // 16) : (h + 1) * (M // 16)]
-            nc.vector.tensor_tensor(window[c][:].indirect(piece_offsets), sig_o[:], tanh_cell[:], MULT)
-            if h == HALVES - 1:
-                nc.sync.dma_start(out[c * P : (c + 1) * P, :], window[c][:])
+            nc.vector.tensor_tensor(window[c][:].indirect(offsets[:]), sig_o[:], tanh_cell[:], MULT)
+            nc.sync.dma_start(out[c * P : (c + 1) * P, :], window[c][:])
 
-        ahead = make_cell(*pieces[0])
-        for i, piece in enumerate(pieces):
-            current = ahead
-            if i + 1 < len(pieces):
-                ahead = make_cell(*pieces[i + 1])
-            place(*piece, current)
+        cells = [make_cell(c) for c in range(C_BLOCKS)]
+        for c in range(C_BLOCKS):
+            place(c, cells[c])

@@ -74,13 +74,27 @@ def tile_treemodel_s_kernel(tc, base, x, w_iou, b_iou, offs, out):
             nc.vector.tensor_tensor(cell[:], sig_i[:], tanh_u[:], MULT)
             return cell
 
-        def place(c, cell):
+        def factors(c, cell):
             sig_o = gate(c, GATE_O, SIGMOID, "sig_o")
             tanh_cell = work.tile([P, N], F32, name="tanh_cell")
             nc.scalar.activation(tanh_cell[:], cell[:], TANH)
-            nc.vector.tensor_tensor(window[c][:].indirect(offsets[:]), sig_o[:], tanh_cell[:], MULT)
+            return sig_o, tanh_cell
+
+        def place(c, sig_o, tanh_cell, first, last):
+            nc.vector.tensor_tensor(
+                window[c][:].indirect(offsets[:, first // 16 : last // 16]),
+                sig_o[:, first:last], tanh_cell[:, first:last], MULT,
+            )
+
+        def store(c):
             nc.sync.dma_start(out[c * P : (c + 1) * P, :], window[c][:])
 
-        cells = [make_cell(c) for c in range(C_BLOCKS)]
-        for c in range(C_BLOCKS):
-            place(c, cells[c])
+        cell0 = make_cell(0)
+        sig_o0, tanh_cell0 = factors(0, cell0)
+        place(0, sig_o0, tanh_cell0, 0, N // 2)
+        cell1 = make_cell(1)
+        place(0, sig_o0, tanh_cell0, N // 2, N)
+        store(0)
+        sig_o1, tanh_cell1 = factors(1, cell1)
+        place(1, sig_o1, tanh_cell1, 0, N)
+        store(1)

@@ -18,13 +18,16 @@ FLOPS = 2 * X * 3 * H * N
 
 WARM_MATMULS = 16
 
+FIRST_PIECE = 64
+UNITS = ((0, 0, FIRST_PIECE), (0, FIRST_PIECE, N), (1, 0, N))
+
 
 def tile_treemodel_s_kernel(tc, base, x, w_iou, b_iou, offs, out):
     nc = tc.nc
     with (
         tc.tile_pool(name="held", bufs=1) as held,
-        tc.tile_pool(name="work", bufs=C_BLOCKS) as work,
-        tc.psum_pool(name="psum", bufs=C_BLOCKS) as psum,
+        tc.tile_pool(name="work", bufs=len(UNITS)) as work,
+        tc.psum_pool(name="psum", bufs=2) as psum,
         tc.psum_pool(name="psum_idle", bufs=1) as psum_idle,
     ):
         offsets = held.tile([P, N // 16], U16, name="offsets")
@@ -32,9 +35,6 @@ def tile_treemodel_s_kernel(tc, base, x, w_iou, b_iou, offs, out):
         x_sb = held.tile([P, K_BLOCKS, N], BF16, name="x_sb")
         w_sb = [held.tile([P, K_BLOCKS, H], BF16, name=f"w_sb{g}") for g in range(3)]
         window = [held.tile([P, S], F32, name=f"window{c}") for c in range(C_BLOCKS)]
-
-        with nc.allow_non_contiguous_dma(reason="768 biases, one to a partition and column"):
-            nc.scalar.dma_start(bias[:], b_iou.rearrange("(r p) o -> p (r o)", p=P))
 
         warm = held.tile([P, 1], F32, name="warm")
         nc.gpsimd.memset(warm[:], 0.0)
@@ -48,53 +48,48 @@ def tile_treemodel_s_kernel(tc, base, x, w_iou, b_iou, offs, out):
 
         w_blocks = w_iou.rearrange("(k p) c -> p k c", p=P)
         nc.sync.dma_start(x_sb[:], x.rearrange("(k p) j -> p k j", p=P))
-        for g in (GATE_I, GATE_U, GATE_O):
+        nc.sync.dma_start(w_sb[GATE_I][:], w_blocks[:, :, GATE_I * H : (GATE_I + 1) * H])
+        with nc.allow_non_contiguous_dma(reason="768 biases, one to a partition and column"):
+            nc.sync.dma_start(bias[:], b_iou.rearrange("(r p) o -> p (r o)", p=P))
+        for g in (GATE_U, GATE_O):
             nc.sync.dma_start(w_sb[g][:], w_blocks[:, :, g * H : (g + 1) * H])
         nc.sync.dma_start(offsets[:], offs)
 
         for c in range(C_BLOCKS):
             nc.gpsimd.dma_start(window[c][:], base[c * P : (c + 1) * P, :])
 
-        def gate(c, g, func, name):
-            pre = psum.tile([P, N], F32, name="pre_" + name)
+        def gate(unit, g, func, name):
+            c, first, last = unit
+            pre = psum.tile([P, last - first], F32, name="pre_" + name)
             for k in range(K_BLOCKS):
                 nc.tensor.matmul(
-                    pre[:], w_sb[g][:, k, c * P : (c + 1) * P], x_sb[:, k, :],
+                    pre[:], w_sb[g][:, k, c * P : (c + 1) * P], x_sb[:, k, first:last],
                     start=(k == 0), stop=(k == K_BLOCKS - 1),
                 )
-            act = work.tile([P, N], F32, name=name)
+            act = work.tile([P, last - first], F32, name=name)
             column = g * C_BLOCKS + c
             nc.scalar.activation(act[:], pre[:], func, bias=bias[:, column : column + 1])
             return act
 
-        def make_cell(c):
-            sig_i = gate(c, GATE_I, SIGMOID, "sig_i")
-            tanh_u = gate(c, GATE_U, TANH, "tanh_u")
-            cell = work.tile([P, N], F32, name="cell")
+        def make_cell(unit):
+            c, first, last = unit
+            sig_i = gate(unit, GATE_I, SIGMOID, "sig_i")
+            tanh_u = gate(unit, GATE_U, TANH, "tanh_u")
+            cell = work.tile([P, last - first], F32, name="cell")
             nc.vector.tensor_tensor(cell[:], sig_i[:], tanh_u[:], MULT)
             return cell
 
-        def factors(c, cell):
-            sig_o = gate(c, GATE_O, SIGMOID, "sig_o")
-            tanh_cell = work.tile([P, N], F32, name="tanh_cell")
+        def place(unit, cell):
+            c, first, last = unit
+            sig_o = gate(unit, GATE_O, SIGMOID, "sig_o")
+            tanh_cell = work.tile([P, last - first], F32, name="tanh_cell")
             nc.scalar.activation(tanh_cell[:], cell[:], TANH)
-            return sig_o, tanh_cell
-
-        def place(c, sig_o, tanh_cell, first, last):
             nc.vector.tensor_tensor(
-                window[c][:].indirect(offsets[:, first // 16 : last // 16]),
-                sig_o[:, first:last], tanh_cell[:, first:last], MULT,
+                window[c][:].indirect(offsets[:, first // 16 : last // 16]), sig_o[:], tanh_cell[:], MULT
             )
+            if last == N:
+                nc.sync.dma_start(out[c * P : (c + 1) * P, :], window[c][:])
 
-        def store(c):
-            nc.sync.dma_start(out[c * P : (c + 1) * P, :], window[c][:])
-
-        cell0 = make_cell(0)
-        sig_o0, tanh_cell0 = factors(0, cell0)
-        place(0, sig_o0, tanh_cell0, 0, N // 2)
-        cell1 = make_cell(1)
-        place(0, sig_o0, tanh_cell0, N // 2, N)
-        store(0)
-        sig_o1, tanh_cell1 = factors(1, cell1)
-        place(1, sig_o1, tanh_cell1, 0, N)
-        store(1)
+        cells = [make_cell(unit) for unit in UNITS]
+        for unit, cell in zip(UNITS, cells):
+            place(unit, cell)

@@ -13,6 +13,7 @@ N = 256
 K_BLOCKS = X // P
 C_BLOCKS = H // P
 GATE_I, GATE_O, GATE_U = 0, 1, 2
+BLOCK_F32 = 8
 
 FLOPS = 2 * X * 3 * H * N
 
@@ -31,7 +32,7 @@ def tile_treemodel_s_kernel(tc, base, x, w_iou, b_iou, offs, out):
         tc.psum_pool(name="psum_idle", bufs=1) as psum_idle,
     ):
         offsets = held.tile([P, N // 16], U16, name="offsets")
-        bias = held.tile([P, 3 * C_BLOCKS], F32, name="bias")
+        bias = held.tile([P, 3 * C_BLOCKS, BLOCK_F32], F32, name="bias")
         x_sb = held.tile([P, K_BLOCKS, N], BF16, name="x_sb")
         w_sb = [held.tile([P, K_BLOCKS, H], BF16, name=f"w_sb{g}") for g in range(3)]
         window = [held.tile([P, S], F32, name=f"window{c}") for c in range(C_BLOCKS)]
@@ -50,7 +51,7 @@ def tile_treemodel_s_kernel(tc, base, x, w_iou, b_iou, offs, out):
         nc.sync.dma_start(x_sb[:], x.rearrange("(k p) j -> p k j", p=P))
         nc.sync.dma_start(w_sb[GATE_I][:], w_blocks[:, :, GATE_I * H : (GATE_I + 1) * H])
         with nc.allow_non_contiguous_dma(reason="768 biases, one to a partition and column"):
-            nc.sync.dma_start(bias[:], b_iou.rearrange("(r p) o -> p (r o)", p=P))
+            nc.sync.dma_start(bias[:, :, 0:1], b_iou.rearrange("(r p) o -> p r o", p=P))
         for g in (GATE_U, GATE_O):
             nc.sync.dma_start(w_sb[g][:], w_blocks[:, :, g * H : (g + 1) * H])
         nc.sync.dma_start(offsets[:], offs)
@@ -67,8 +68,7 @@ def tile_treemodel_s_kernel(tc, base, x, w_iou, b_iou, offs, out):
                     start=(k == 0), stop=(k == K_BLOCKS - 1),
                 )
             act = work.tile([P, last - first], F32, name=name)
-            column = g * C_BLOCKS + c
-            nc.scalar.activation(act[:], pre[:], func, bias=bias[:, column : column + 1])
+            nc.scalar.activation(act[:], pre[:], func, bias=bias[:, g * C_BLOCKS + c, 0:1])
             return act
 
         def make_cell(unit):

@@ -34,7 +34,8 @@ def tile_treemodel_s_kernel(tc, base, x, w_iou, b_iou, offs, out):
         offsets = held.tile([P, N // 16], U16, name="offsets")
         bias = held.tile([P, 3 * C_BLOCKS, BLOCK_F32], F32, name="bias")
         x_sb = held.tile([P, K_BLOCKS, N], BF16, name="x_sb")
-        w_sb = [held.tile([P, K_BLOCKS, H], BF16, name=f"w_sb{g}") for g in range(3)]
+        w_cell = [held.tile([P, 2, H], BF16, name=f"w_cell{k}") for k in range(K_BLOCKS)]
+        w_out = held.tile([P, K_BLOCKS, H], BF16, name="w_out")
         window = [held.tile([P, S], F32, name=f"window{c}") for c in range(C_BLOCKS)]
 
         warm = held.tile([P, 1], F32, name="warm")
@@ -47,13 +48,13 @@ def tile_treemodel_s_kernel(tc, base, x, w_iou, b_iou, offs, out):
         for repeat in range(WARM_MATMULS):
             nc.tensor.matmul(idle[:], zeros[:], zeros[:], start=True, stop=True)
 
-        w_blocks = w_iou.rearrange("(k p) c -> p k c", p=P)
+        w_gates = w_iou.rearrange("(k p) (g c) -> p k g c", p=P, g=3)
         nc.sync.dma_start(x_sb[:], x.rearrange("(k p) j -> p k j", p=P))
-        nc.sync.dma_start(w_sb[GATE_I][:], w_blocks[:, :, GATE_I * H : (GATE_I + 1) * H])
+        for k in range(K_BLOCKS):
+            nc.sync.dma_start(w_cell[k][:], w_gates[:, k, GATE_I : GATE_U + 1 : GATE_U - GATE_I, :])
         with nc.allow_non_contiguous_dma(reason="768 biases, one to a partition and column"):
             nc.sync.dma_start(bias[:, :, 0:1], b_iou.rearrange("(r p) o -> p r o", p=P))
-        for g in (GATE_U, GATE_O):
-            nc.sync.dma_start(w_sb[g][:], w_blocks[:, :, g * H : (g + 1) * H])
+        nc.sync.dma_start(w_out[:], w_gates[:, :, GATE_O, :])
         nc.sync.dma_start(offsets[:], offs)
 
         for c in range(C_BLOCKS):
@@ -61,12 +62,14 @@ def tile_treemodel_s_kernel(tc, base, x, w_iou, b_iou, offs, out):
 
         def gate(unit, g, func, name):
             c, first, last = unit
+            weights = {
+                GATE_I: [w_cell[k][:, 0, c * P : (c + 1) * P] for k in range(K_BLOCKS)],
+                GATE_U: [w_cell[k][:, 1, c * P : (c + 1) * P] for k in range(K_BLOCKS)],
+                GATE_O: [w_out[:, k, c * P : (c + 1) * P] for k in range(K_BLOCKS)],
+            }[g]
             pre = psum.tile([P, last - first], F32, name="pre_" + name)
             for k in range(K_BLOCKS):
-                nc.tensor.matmul(
-                    pre[:], w_sb[g][:, k, c * P : (c + 1) * P], x_sb[:, k, first:last],
-                    start=(k == 0), stop=(k == K_BLOCKS - 1),
-                )
+                nc.tensor.matmul(pre[:], weights[k], x_sb[:, k, first:last], start=(k == 0), stop=(k == K_BLOCKS - 1))
             act = work.tile([P, last - first], F32, name=name)
             nc.scalar.activation(act[:], pre[:], func, bias=bias[:, g * C_BLOCKS + c, 0:1])
             return act
@@ -90,6 +93,7 @@ def tile_treemodel_s_kernel(tc, base, x, w_iou, b_iou, offs, out):
             if last == N:
                 nc.sync.dma_start(out[c * P : (c + 1) * P, :], window[c][:])
 
-        cells = [make_cell(unit) for unit in UNITS]
-        for unit, cell in zip(UNITS, cells):
+        place(UNITS[0], make_cell(UNITS[0]))
+        cells = [make_cell(unit) for unit in UNITS[1:]]
+        for unit, cell in zip(UNITS[1:], cells):
             place(unit, cell)

@@ -20,7 +20,7 @@ FLOPS = 2 * X * 3 * H * N
 WARM_MATMULS = 16
 
 FIRST_PIECE = 64
-UNITS = ((0, 0, FIRST_PIECE), (0, FIRST_PIECE, N), (1, 0, N))
+UNITS = ((0, 0, FIRST_PIECE), (1, 0, N // 2), (0, FIRST_PIECE, N), (1, N // 2, N))
 
 
 def tile_treemodel_s_kernel(tc, base, x, w_iou, b_iou, offs, out):
@@ -93,7 +93,8 @@ def tile_treemodel_s_kernel(tc, base, x, w_iou, b_iou, offs, out):
             if last == N:
                 nc.sync.dma_start(out[c * P : (c + 1) * P, :], window[c][:])
 
-        place(UNITS[0], make_cell(UNITS[0]))
-        cells = [make_cell(unit) for unit in UNITS[1:]]
-        for unit, cell in zip(UNITS[1:], cells):
-            place(unit, cell)
+        cells = [make_cell(UNITS[0])]
+        for n, unit in enumerate(UNITS):
+            if n + 1 < len(UNITS):
+                cells.append(make_cell(UNITS[n + 1]))
+            place(unit, cells[n])

@@ -32,7 +32,7 @@ def tile_treemodel_s_kernel(tc, base, x, w_iou, b_iou, offs, out):
         tc.psum_pool(name="psum_idle", bufs=1) as psum_idle,
     ):
         offsets = held.tile([P, N // 16], U16, name="offsets")
-        bias = held.tile([P, 3 * C_BLOCKS, BLOCK_F32], F32, name="bias")
+        bias = held.tile([P, 3, BLOCK_F32], F32, name="bias")
         x_sb = held.tile([P, K_BLOCKS, N], BF16, name="x_sb")
         w_cell = [held.tile([P, 2, H], BF16, name=f"w_cell{k}") for k in range(K_BLOCKS)]
         w_out = held.tile([P, K_BLOCKS, H], BF16, name="w_out")
@@ -52,26 +52,28 @@ def tile_treemodel_s_kernel(tc, base, x, w_iou, b_iou, offs, out):
         nc.sync.dma_start(x_sb[:], x.rearrange("(k p) j -> p k j", p=P))
         for k in range(K_BLOCKS):
             nc.sync.dma_start(w_cell[k][:], w_gates[:, k, GATE_I : GATE_U + 1 : GATE_U - GATE_I, :])
-        with nc.allow_non_contiguous_dma(reason="768 biases, one to a partition and column"):
-            nc.sync.dma_start(bias[:, :, 0:1], b_iou.rearrange("(r p) o -> p r o", p=P))
+        with nc.allow_non_contiguous_dma(reason="768 biases, two to a partition and gate"):
+            nc.sync.dma_start(bias[:, :, 0:C_BLOCKS], b_iou.rearrange("(g p c) o -> p g (c o)", p=P, c=C_BLOCKS))
         nc.sync.dma_start(w_out[:], w_gates[:, :, GATE_O, :])
         nc.sync.dma_start(offsets[:], offs)
 
+        base_blocks = base.rearrange("(p c) s -> p c s", c=C_BLOCKS)
+        out_blocks = out.rearrange("(p c) s -> p c s", c=C_BLOCKS)
         for c in range(C_BLOCKS):
-            nc.gpsimd.dma_start(window[c][:], base[c * P : (c + 1) * P, :])
+            nc.gpsimd.dma_start(window[c][:], base_blocks[:, c, :])
 
         def gate(unit, g, func, name):
             c, first, last = unit
             weights = {
-                GATE_I: [w_cell[k][:, 0, c * P : (c + 1) * P] for k in range(K_BLOCKS)],
-                GATE_U: [w_cell[k][:, 1, c * P : (c + 1) * P] for k in range(K_BLOCKS)],
-                GATE_O: [w_out[:, k, c * P : (c + 1) * P] for k in range(K_BLOCKS)],
+                GATE_I: [w_cell[k][:, 0, c:H:C_BLOCKS] for k in range(K_BLOCKS)],
+                GATE_U: [w_cell[k][:, 1, c:H:C_BLOCKS] for k in range(K_BLOCKS)],
+                GATE_O: [w_out[:, k, c:H:C_BLOCKS] for k in range(K_BLOCKS)],
             }[g]
             pre = psum.tile([P, last - first], F32, name="pre_" + name)
             for k in range(K_BLOCKS):
                 nc.tensor.matmul(pre[:], weights[k], x_sb[:, k, first:last], start=(k == 0), stop=(k == K_BLOCKS - 1))
             act = work.tile([P, last - first], F32, name=name)
-            nc.scalar.activation(act[:], pre[:], func, bias=bias[:, g * C_BLOCKS + c, 0:1])
+            nc.scalar.activation(act[:], pre[:], func, bias=bias[:, g, c : c + 1])
             return act
 
         def make_cell(unit):
@@ -91,7 +93,7 @@ def tile_treemodel_s_kernel(tc, base, x, w_iou, b_iou, offs, out):
                 window[c][:].indirect(offsets[:, first // 16 : last // 16]), sig_o[:], tanh_cell[:], MULT
             )
             if last == N:
-                nc.sync.dma_start(out[c * P : (c + 1) * P, :], window[c][:])
+                nc.sync.dma_start(out_blocks[:, c, :], window[c][:])
 
         cells = [make_cell(UNITS[0])]
         for n, unit in enumerate(UNITS):

@@ -17,9 +17,9 @@ BLOCK_F32 = 8
 
 FLOPS = 2 * X * 3 * H * N
 
-WARM_MATMULS = 16
+WARM_MATMULS = 12
 
-FIRST_PIECE = 64
+FIRST_PIECE = 96
 UNITS = ((0, 0, FIRST_PIECE), (1, 0, N // 2), (0, FIRST_PIECE, N), (1, N // 2, N))
 
 

import concourse.mybir as mybir

BF16, F32, U16 = mybir.dt.bfloat16, mybir.dt.float32, mybir.dt.uint16
SIGMOID = mybir.ActivationFunctionType.Sigmoid
TANH = mybir.ActivationFunctionType.Tanh
MULT = mybir.AluOpType.mult

P = 128
X = 256
H = 256
S = 512
N = 256
K_BLOCKS = X // P
C_BLOCKS = H // P
GATE_I, GATE_O, GATE_U = 0, 1, 2
BLOCK_F32 = 8

FLOPS = 2 * X * 3 * H * N

WARM_MATMULS = 12

FIRST_PIECE = 96
UNITS = ((0, 0, FIRST_PIECE), (1, 0, N // 2), (0, FIRST_PIECE, N), (1, N // 2, N))


def tile_treemodel_s_kernel(tc, base, x, w_iou, b_iou, offs, out):
    nc = tc.nc
    with (
        tc.tile_pool(name="held", bufs=1) as held,
        tc.tile_pool(name="work", bufs=len(UNITS)) as work,
        tc.psum_pool(name="psum", bufs=2) as psum,
        tc.psum_pool(name="psum_idle", bufs=1) as psum_idle,
    ):
        offsets = held.tile([P, N // 16], U16, name="offsets")
        bias = held.tile([P, 3, BLOCK_F32], F32, name="bias")
        x_sb = held.tile([P, K_BLOCKS, N], BF16, name="x_sb")
        w_cell = [held.tile([P, 2, H], BF16, name=f"w_cell{k}") for k in range(K_BLOCKS)]
        w_out = held.tile([P, K_BLOCKS, H], BF16, name="w_out")
        window = [held.tile([P, S], F32, name=f"window{c}") for c in range(C_BLOCKS)]

        warm = held.tile([P, 1], F32, name="warm")
        nc.gpsimd.memset(warm[:], 0.0)
        nc.scalar.activation(warm[:], warm[:], SIGMOID)

        zeros = held.tile([P, P], BF16, name="zeros")
        nc.vector.memset(zeros[:], 0.0)
        idle = psum_idle.tile([P, P], F32, name="idle")
        for repeat in range(WARM_MATMULS):
            nc.tensor.matmul(idle[:], zeros[:], zeros[:], start=True, stop=True)

        w_gates = w_iou.rearrange("(k p) (g c) -> p k g c", p=P, g=3)
        nc.sync.dma_start(x_sb[:], x.rearrange("(k p) j -> p k j", p=P))
        for k in range(K_BLOCKS):
            nc.sync.dma_start(w_cell[k][:], w_gates[:, k, GATE_I : GATE_U + 1 : GATE_U - GATE_I, :])
        with nc.allow_non_contiguous_dma(reason="768 biases, two to a partition and gate"):
            nc.sync.dma_start(bias[:, :, 0:C_BLOCKS], b_iou.rearrange("(g p c) o -> p g (c o)", p=P, c=C_BLOCKS))
        nc.sync.dma_start(w_out[:], w_gates[:, :, GATE_O, :])
        nc.sync.dma_start(offsets[:], offs)

        base_blocks = base.rearrange("(p c) s -> p c s", c=C_BLOCKS)
        out_blocks = out.rearrange("(p c) s -> p c s", c=C_BLOCKS)
        for c in range(C_BLOCKS):
            nc.gpsimd.dma_start(window[c][:], base_blocks[:, c, :])

        def gate(unit, g, func, name):
            c, first, last = unit
            weights = {
                GATE_I: [w_cell[k][:, 0, c:H:C_BLOCKS] for k in range(K_BLOCKS)],
                GATE_U: [w_cell[k][:, 1, c:H:C_BLOCKS] for k in range(K_BLOCKS)],
                GATE_O: [w_out[:, k, c:H:C_BLOCKS] for k in range(K_BLOCKS)],
            }[g]
            pre = psum.tile([P, last - first], F32, name="pre_" + name)
            for k in range(K_BLOCKS):
                nc.tensor.matmul(pre[:], weights[k], x_sb[:, k, first:last], start=(k == 0), stop=(k == K_BLOCKS - 1))
            act = work.tile([P, last - first], F32, name=name)
            nc.scalar.activation(act[:], pre[:], func, bias=bias[:, g, c : c + 1])
            return act

        def make_cell(unit):
            c, first, last = unit
            sig_i = gate(unit, GATE_I, SIGMOID, "sig_i")
            tanh_u = gate(unit, GATE_U, TANH, "tanh_u")
            cell = work.tile([P, last - first], F32, name="cell")
            nc.vector.tensor_tensor(cell[:], sig_i[:], tanh_u[:], MULT)
            return cell

        def place(unit, cell):
            c, first, last = unit
            sig_o = gate(unit, GATE_O, SIGMOID, "sig_o")
            tanh_cell = work.tile([P, last - first], F32, name="tanh_cell")
            nc.scalar.activation(tanh_cell[:], cell[:], TANH)
            nc.vector.tensor_tensor(
                window[c][:].indirect(offsets[:, first // 16 : last // 16]), sig_o[:], tanh_cell[:], MULT
            )
            if last == N:
                nc.sync.dma_start(out_blocks[:, c, :], window[c][:])

        cells = [make_cell(UNITS[0])]
        for n, unit in enumerate(UNITS):
            if n + 1 < len(UNITS):
                cells.append(make_cell(UNITS[n + 1]))
            place(unit, cells[n])
